import numpy as np
import ml_dtypes

BF16 = ml_dtypes.bfloat16


def bf(x):
    return np.asarray(x, np.float32).astype(BF16)


def f32(x):
    return np.asarray(x, np.float32)


def f64(x):
    return np.asarray(x).astype(np.float64)


def striped(idx):
    return np.tile(idx.reshape(-1, 16).T, (8, 1))


S, D, T, N = 4096, 128, 4096, 2048


def setup_inputs():
    z = np.random.standard_normal((D, T))
    z = (z - z.mean(0, keepdims=True)) / z.std(0, keepdims=True)
    return {"x": f32(z), "table": bf(np.random.standard_normal((S, D))), "wq": bf(np.random.standard_normal((D, D)) / np.sqrt(D)), "bq": f32(0.1 * np.random.standard_normal((D, 1))), "wk": bf(np.random.standard_normal((D, D)) / np.sqrt(D)), "bk": f32(0.1 * np.random.standard_normal((D, 1))), "wv": bf(np.random.standard_normal((D, D)) / np.sqrt(D)), "bv": f32(0.1 * np.random.standard_normal((D, 1))), "offs": striped(np.random.permutation(S)[:N])}


def reference(x, table, wq, bq, wk, bk, wv, bv, offs):
    idx = offs[:16].T.reshape(-1)
    tags = f64(table)[idx].T
    k = f64(wk).T @ tags + f64(bk)
    v = f64(wv).T @ tags + f64(bv)
    q = f64(wq).T @ f64(x) + f64(bq)
    s = q.T @ k / np.sqrt(D)
    return np.concatenate([v, s], axis=0)

@@ -1,0 +1,116 @@
+import math
+
+import concourse.masks as masks
+import concourse.mybir as mybir
+
+P = 128
+WORDS = 4096
+TOKENS = 4096
+N = 2048
+PIECE = 512
+FLIP = 4
+BF16, F32, U16 = mybir.dt.bfloat16, mybir.dt.float32, mybir.dt.uint16
+
+FLOPS = 2 * P * P * (2 * N + TOKENS) + 2 * P * TOKENS * N
+
+
+def tile_entattentionlayer_b_kernel(tc, x, table, wq, bq, wk, bk, wv, bv, offs, out):
+    nc = tc.nc
+    identity_fn = mybir.ActivationFunctionType.Identity
+    add, mult = mybir.AluOpType.add, mybir.AluOpType.mult
+    inv_sqrt_d = 1.0 / math.sqrt(P)
+
+    with (
+        tc.tile_pool(name="held", bufs=1) as held,
+        tc.tile_pool(name="staging", bufs=6) as staging,
+        tc.psum_pool(name="flip", bufs=2) as flip,
+        tc.psum_pool(name="banks", bufs=6) as banks,
+    ):
+        offsets = held.tile([P, N // 16], U16, name="offsets")
+        nc.sync.dma_start(offsets[:], offs)
+
+        weights = {}
+        biases = {}
+        for name, w_dram, b_dram in (("q", wq, bq), ("k", wk, bk), ("v", wv, bv)):
+            weights[name] = held.tile([P, P], BF16, name=f"w{name}")
+            nc.scalar.dma_start(weights[name][:], w_dram)
+            biases[name] = held.tile([P, 1], F32, name=f"b{name}")
+            nc.scalar.dma_start(biases[name][:], b_dram)
+
+        x_f32 = held.tile([P, TOKENS], F32, name="x_f32")
+        nc.scalar.dma_start(x_f32[:, 0:PIECE], x[:, 0:PIECE])
+
+        table_blocks = table.rearrange("(b p) d -> p b d", p=P)
+        word_rows = held.tile([P, WORDS // P, P], BF16, name="word_rows")
+        for g in range(WORDS // P // FLIP):
+            blocks = slice(g * FLIP, (g + 1) * FLIP)
+            nc.sync.dma_start(word_rows[:, blocks, :], table_blocks[:, blocks, :])
+
+        for c in range(1, TOKENS // PIECE):
+            cols = slice(c * PIECE, (c + 1) * PIECE)
+            nc.sync.dma_start(x_f32[:, cols], x[:, cols])
+
+        identity = held.tile([P, P], BF16, name="identity")
+        masks.make_identity(nc, identity[:])
+
+        def add_bias(turn, dest, bank, bias):
+            if turn % 2 == 0:
+                nc.vector.tensor_scalar(dest, bank, bias, None, add)
+            else:
+                nc.scalar.activation(dest, bank, identity_fn, bias=bias)
+
+        def scale_down(turn, dest, bank):
+            if turn % 2 == 0:
+                nc.vector.tensor_scalar(dest, bank, inv_sqrt_d, None, mult)
+            else:
+                nc.scalar.activation(dest, bank, identity_fn, scale=inv_sqrt_d)
+
+        x_bf = held.tile([P, TOKENS], BF16, name="x_bf")
+        q_bf = held.tile([P, TOKENS], BF16, name="q_bf")
+
+        def project_queries(c):
+            cols = slice(c * PIECE, (c + 1) * PIECE)
+            nc.gpsimd.tensor_copy(x_bf[:, cols], x_f32[:, cols])
+            bank = banks.tile([P, PIECE], F32, name="bank")
+            nc.tensor.matmul(bank[:], weights["q"][:], x_bf[:, cols], start=True, stop=True)
+            add_bias(c, q_bf[:, cols], bank[:], biases["q"][:, 0:1])
+
+        project_queries(0)
+
+        window = held.tile([P, WORDS], BF16, name="window")
+        for g in range(WORDS // P // FLIP):
+            flipped = flip.tile([P, FLIP * P], BF16, name="flipped")
+            for b in range(FLIP):
+                nc.tensor.transpose(flipped[:, b * P : (b + 1) * P], word_rows[:, g * FLIP + b, :], identity[:])
+            cols = slice(g * FLIP * P, (g + 1) * FLIP * P)
+            if g % 2 == 0:
+                nc.vector.tensor_copy(window[:, cols], flipped[:])
+            else:
+                nc.scalar.copy(window[:, cols], flipped[:])
+
+        def project_tags(name, j, dest):
+            looked_up = window[:].indirect(offsets[:, j * (PIECE // 16) : (j + 1) * (PIECE // 16)])
+            bank = banks.tile([P, PIECE], F32, name="bank")
+            nc.tensor.matmul(bank[:], weights[name][:], looked_up, start=True, stop=True)
+            add_bias(j, dest, bank[:], biases[name][:, 0:1])
+
+        k_bf = held.tile([P, N], BF16, name="k_bf")
+        for j in range(N // PIECE):
+            project_tags("k", j, k_bf[:, j * PIECE : (j + 1) * PIECE])
+
+        for t in range(TOKENS // P):
+            if t % (PIECE // P) == 0 and t // (PIECE // P) + 1 < TOKENS // PIECE:
+                project_queries(t // (PIECE // P) + 1)
+            rows = staging.tile([P, N], F32, name="rows")
+            for j in range(N // PIECE):
+                cols = slice(j * PIECE, (j + 1) * PIECE)
+                bank = banks.tile([P, PIECE], F32, name="bank")
+                nc.tensor.matmul(bank[:], q_bf[:, t * P : (t + 1) * P], k_bf[:, cols], start=True, stop=True)
+                scale_down(j, rows[:, cols], bank[:])
+            nc.sync.dma_start(out[P + t * P : P + (t + 1) * P, :], rows[:])
+
+            if t == 7:
+                rows = staging.tile([P, N], F32, name="rows")
+                for j in range(N // PIECE):
+                    project_tags("v", j, rows[:, j * PIECE : (j + 1) * PIECE])
+                nc.sync.dma_start(out[0:P, :], rows[:])

@@ -19,39 +19,51 @@ def tile_entattentionlayer_b_kernel(tc, x, table, wq, bq, wk, bk, wv, bv, offs, 
     identity_fn = mybir.ActivationFunctionType.Identity
     add, mult = mybir.AluOpType.add, mybir.AluOpType.mult
     inv_sqrt_d = 1.0 / math.sqrt(P)
+    n_groups = WORDS // P // FLIP
+    n_chunks = TOKENS // PIECE
 
     with (
         tc.tile_pool(name="held", bufs=1) as held,
+        tc.tile_pool(name="landing", bufs=n_groups) as landing,
         tc.tile_pool(name="staging", bufs=6) as staging,
         tc.psum_pool(name="flip", bufs=2) as flip,
         tc.psum_pool(name="banks", bufs=6) as banks,
     ):
+        table_groups = table.rearrange("(g b p) d -> g p b d", b=FLIP, p=P)
+        word_rows = []
+        for g in range(n_groups):
+            word_rows.append(landing.tile([P, FLIP, P], BF16, name="word_rows", tag="landing"))
+            nc.sync.dma_start(word_rows[g][:], table_groups[g])
+
         offsets = held.tile([P, N // 16], U16, name="offsets")
         nc.sync.dma_start(offsets[:], offs)
 
         weights = {}
         biases = {}
-        for name, w_dram, b_dram in (("q", wq, bq), ("k", wk, bk), ("v", wv, bv)):
+        for name, w_dram, b_dram in (("k", wk, bk), ("q", wq, bq), ("v", wv, bv)):
             weights[name] = held.tile([P, P], BF16, name=f"w{name}")
             nc.scalar.dma_start(weights[name][:], w_dram)
             biases[name] = held.tile([P, 1], F32, name=f"b{name}")
             nc.scalar.dma_start(biases[name][:], b_dram)
 
-        x_f32 = held.tile([P, TOKENS], F32, name="x_f32")
-        nc.scalar.dma_start(x_f32[:, 0:PIECE], x[:, 0:PIECE])
-
-        table_blocks = table.rearrange("(b p) d -> p b d", p=P)
-        word_rows = held.tile([P, WORDS // P, P], BF16, name="word_rows")
-        for g in range(WORDS // P // FLIP):
-            blocks = slice(g * FLIP, (g + 1) * FLIP)
-            nc.sync.dma_start(word_rows[:, blocks, :], table_blocks[:, blocks, :])
-
-        for c in range(1, TOKENS // PIECE):
-            cols = slice(c * PIECE, (c + 1) * PIECE)
-            nc.sync.dma_start(x_f32[:, cols], x[:, cols])
-
         identity = held.tile([P, P], BF16, name="identity")
         masks.make_identity(nc, identity[:])
+
+        window = held.tile([P, WORDS], BF16, name="window")
+        for g in range(n_groups):
+            flipped = flip.tile([P, FLIP * P], BF16, name="flipped")
+            for b in range(FLIP):
+                nc.tensor.transpose(flipped[:, b * P : (b + 1) * P], word_rows[g][:, b, :], identity[:])
+            cols = slice(g * FLIP * P, (g + 1) * FLIP * P)
+            if g % 2 == 0:
+                nc.vector.tensor_copy(window[:, cols], flipped[:])
+            else:
+                nc.scalar.copy(window[:, cols], flipped[:])
+
+        x_f32 = []
+        for c in range(n_chunks):
+            x_f32.append(landing.tile([P, PIECE], F32, name="x_f32", tag="landing"))
+            nc.sync.dma_start(x_f32[c][:], x[:, c * PIECE : (c + 1) * PIECE])
 
         def add_bias(turn, dest, bank, bias):
             if turn % 2 == 0:
@@ -70,23 +82,10 @@ def tile_entattentionlayer_b_kernel(tc, x, table, wq, bq, wk, bk, wv, bv, offs, 
 
         def project_queries(c):
             cols = slice(c * PIECE, (c + 1) * PIECE)
-            nc.gpsimd.tensor_copy(x_bf[:, cols], x_f32[:, cols])
+            nc.gpsimd.tensor_copy(x_bf[:, cols], x_f32[c][:])
             bank = banks.tile([P, PIECE], F32, name="bank")
             nc.tensor.matmul(bank[:], weights["q"][:], x_bf[:, cols], start=True, stop=True)
             add_bias(c, q_bf[:, cols], bank[:], biases["q"][:, 0:1])
-
-        project_queries(0)
-
-        window = held.tile([P, WORDS], BF16, name="window")
-        for g in range(WORDS // P // FLIP):
-            flipped = flip.tile([P, FLIP * P], BF16, name="flipped")
-            for b in range(FLIP):
-                nc.tensor.transpose(flipped[:, b * P : (b + 1) * P], word_rows[:, g * FLIP + b, :], identity[:])
-            cols = slice(g * FLIP * P, (g + 1) * FLIP * P)
-            if g % 2 == 0:
-                nc.vector.tensor_copy(window[:, cols], flipped[:])
-            else:
-                nc.scalar.copy(window[:, cols], flipped[:])
 
         def project_tags(name, j, dest):
             looked_up = window[:].indirect(offsets[:, j * (PIECE // 16) : (j + 1) * (PIECE // 16)])
@@ -94,13 +93,13 @@ def tile_entattentionlayer_b_kernel(tc, x, table, wq, bq, wk, bk, wv, bv, offs, 
             nc.tensor.matmul(bank[:], weights[name][:], looked_up, start=True, stop=True)
             add_bias(j, dest, bank[:], biases[name][:, 0:1])
 
+        project_queries(0)
+
         k_bf = held.tile([P, N], BF16, name="k_bf")
         for j in range(N // PIECE):
             project_tags("k", j, k_bf[:, j * PIECE : (j + 1) * PIECE])
 
         for t in range(TOKENS // P):
-            if t % (PIECE // P) == 0 and t // (PIECE // P) + 1 < TOKENS // PIECE:
-                project_queries(t // (PIECE // P) + 1)
             rows = staging.tile([P, N], F32, name="rows")
             for j in range(N // PIECE):
                 cols = slice(j * PIECE, (j + 1) * PIECE)
@@ -108,6 +107,9 @@ def tile_entattentionlayer_b_kernel(tc, x, table, wq, bq, wk, bk, wv, bv, offs, 
                 nc.tensor.matmul(bank[:], q_bf[:, t * P : (t + 1) * P], k_bf[:, cols], start=True, stop=True)
                 scale_down(j, rows[:, cols], bank[:])
             nc.sync.dma_start(out[P + t * P : P + (t + 1) * P, :], rows[:])
+
+            if t % (PIECE // P) == 0 and t // (PIECE // P) + 1 < n_chunks:
+                project_queries(t // (PIECE // P) + 1)
 
             if t == 7:
                 rows = staging.tile([P, N], F32, name="rows")

@@ -8,6 +8,7 @@ WORDS = 4096
 TOKENS = 4096
 N = 2048
 PIECE = 512
+GROUP = PIECE // P
 FLIP = 4
 BF16, F32, U16 = mybir.dt.bfloat16, mybir.dt.float32, mybir.dt.uint16
 
@@ -25,7 +26,7 @@ def tile_entattentionlayer_b_kernel(tc, x, table, wq, bq, wk, bk, wv, bv, offs, 
     with (
         tc.tile_pool(name="held", bufs=1) as held,
         tc.tile_pool(name="landing", bufs=n_groups) as landing,
-        tc.tile_pool(name="staging", bufs=6) as staging,
+        tc.tile_pool(name="staging", bufs=3) as staging,
         tc.psum_pool(name="flip", bufs=2) as flip,
         tc.psum_pool(name="banks", bufs=6) as banks,
     ):
@@ -99,20 +100,26 @@ def tile_entattentionlayer_b_kernel(tc, x, table, wq, bq, wk, bk, wv, bv, offs, 
         for j in range(N // PIECE):
             project_tags("k", j, k_bf[:, j * PIECE : (j + 1) * PIECE])
 
-        for t in range(TOKENS // P):
-            rows = staging.tile([P, N], F32, name="rows")
-            for j in range(N // PIECE):
-                cols = slice(j * PIECE, (j + 1) * PIECE)
-                bank = banks.tile([P, PIECE], F32, name="bank")
-                nc.tensor.matmul(bank[:], q_bf[:, t * P : (t + 1) * P], k_bf[:, cols], start=True, stop=True)
-                scale_down(j, rows[:, cols], bank[:])
-            nc.sync.dma_start(out[P + t * P : P + (t + 1) * P, :], rows[:])
-
-            if t % (PIECE // P) == 0 and t // (PIECE // P) + 1 < n_chunks:
-                project_queries(t // (PIECE // P) + 1)
-
-            if t == 7:
-                rows = staging.tile([P, N], F32, name="rows")
+        for c in range(n_chunks):
+            rows = staging.tile([P, GROUP, N], F32, name="rows")
+            out_rows = out[P + c * PIECE : P + (c + 1) * PIECE, :].rearrange("(i p) n -> p i n", p=P)
+            by_block = c == 0 or c == n_chunks - 1
+            for i in range(GROUP):
+                t = c * GROUP + i
                 for j in range(N // PIECE):
-                    project_tags("v", j, rows[:, j * PIECE : (j + 1) * PIECE])
-                nc.sync.dma_start(out[0:P, :], rows[:])
+                    cols = slice(j * PIECE, (j + 1) * PIECE)
+                    bank = banks.tile([P, PIECE], F32, name="bank")
+                    nc.tensor.matmul(bank[:], q_bf[:, t * P : (t + 1) * P], k_bf[:, cols], start=True, stop=True)
+                    scale_down(j, rows[:, i, cols], bank[:])
+                if by_block:
+                    nc.sync.dma_start(out_rows[:, i, :], rows[:, i, :])
+                if i == 0 and c + 1 < n_chunks:
+                    project_queries(c + 1)
+            if not by_block:
+                nc.sync.dma_start(out_rows, rows[:])
+
+            if c == 1:
+                v_rows = held.tile([P, N], F32, name="v_rows")
+                for j in range(N // PIECE):
+                    project_tags("v", j, v_rows[:, j * PIECE : (j + 1) * PIECE])
+                nc.sync.dma_start(out[0:P, :], v_rows[:])

@@ -8,7 +8,7 @@ WORDS = 4096
 TOKENS = 4096
 N = 2048
 PIECE = 512
-GROUP = PIECE // P
+WARM_UP = 5
 FLIP = 4
 BF16, F32, U16 = mybir.dt.bfloat16, mybir.dt.float32, mybir.dt.uint16
 
@@ -26,7 +26,7 @@ def tile_entattentionlayer_b_kernel(tc, x, table, wq, bq, wk, bk, wv, bv, offs, 
     with (
         tc.tile_pool(name="held", bufs=1) as held,
         tc.tile_pool(name="landing", bufs=n_groups) as landing,
-        tc.tile_pool(name="staging", bufs=3) as staging,
+        tc.tile_pool(name="staging", bufs=6) as staging,
         tc.psum_pool(name="flip", bufs=2) as flip,
         tc.psum_pool(name="banks", bufs=6) as banks,
     ):
@@ -50,11 +50,22 @@ def tile_entattentionlayer_b_kernel(tc, x, table, wq, bq, wk, bk, wv, bv, offs, 
         identity = held.tile([P, P], BF16, name="identity")
         masks.make_identity(nc, identity[:])
 
+        zeros = held.tile([P, PIECE], BF16, name="zeros")
+        nc.vector.memset(zeros[:], 0.0)
+
+        def keep_warm(moving):
+            unread = banks.tile([P, PIECE], F32, name="bank")
+            nc.tensor.matmul(unread[:], zeros[:, 0:P], moving, start=True, stop=True)
+
+        for w in range(WARM_UP):
+            keep_warm(zeros[:])
+
         window = held.tile([P, WORDS], BF16, name="window")
         for g in range(n_groups):
             flipped = flip.tile([P, FLIP * P], BF16, name="flipped")
             for b in range(FLIP):
                 nc.tensor.transpose(flipped[:, b * P : (b + 1) * P], word_rows[g][:, b, :], identity[:])
+            keep_warm(word_rows[g][:].rearrange("p b d -> p (b d)"))
             cols = slice(g * FLIP * P, (g + 1) * FLIP * P)
             if g % 2 == 0:
                 nc.vector.tensor_copy(window[:, cols], flipped[:])
@@ -100,26 +111,20 @@ def tile_entattentionlayer_b_kernel(tc, x, table, wq, bq, wk, bk, wv, bv, offs, 
         for j in range(N // PIECE):
             project_tags("k", j, k_bf[:, j * PIECE : (j + 1) * PIECE])
 
-        for c in range(n_chunks):
-            rows = staging.tile([P, GROUP, N], F32, name="rows")
-            out_rows = out[P + c * PIECE : P + (c + 1) * PIECE, :].rearrange("(i p) n -> p i n", p=P)
-            by_block = c == 0 or c == n_chunks - 1
-            for i in range(GROUP):
-                t = c * GROUP + i
-                for j in range(N // PIECE):
-                    cols = slice(j * PIECE, (j + 1) * PIECE)
-                    bank = banks.tile([P, PIECE], F32, name="bank")
-                    nc.tensor.matmul(bank[:], q_bf[:, t * P : (t + 1) * P], k_bf[:, cols], start=True, stop=True)
-                    scale_down(j, rows[:, i, cols], bank[:])
-                if by_block:
-                    nc.sync.dma_start(out_rows[:, i, :], rows[:, i, :])
-                if i == 0 and c + 1 < n_chunks:
-                    project_queries(c + 1)
-            if not by_block:
-                nc.sync.dma_start(out_rows, rows[:])
+        for t in range(TOKENS // P):
+            rows = staging.tile([P, N], F32, name="rows")
+            for j in range(N // PIECE):
+                cols = slice(j * PIECE, (j + 1) * PIECE)
+                bank = banks.tile([P, PIECE], F32, name="bank")
+                nc.tensor.matmul(bank[:], q_bf[:, t * P : (t + 1) * P], k_bf[:, cols], start=True, stop=True)
+                scale_down(j, rows[:, cols], bank[:])
+            nc.sync.dma_start(out[P + t * P : P + (t + 1) * P, :], rows[:])
 
-            if c == 1:
-                v_rows = held.tile([P, N], F32, name="v_rows")
+            if t % (PIECE // P) == 0 and t // (PIECE // P) + 1 < n_chunks:
+                project_queries(t // (PIECE // P) + 1)
+
+            if t == 7:
+                rows = staging.tile([P, N], F32, name="rows")
                 for j in range(N // PIECE):
-                    project_tags("v", j, v_rows[:, j * PIECE : (j + 1) * PIECE])
-                nc.sync.dma_start(out[0:P, :], v_rows[:])
+                    project_tags("v", j, rows[:, j * PIECE : (j + 1) * PIECE])
+                nc.sync.dma_start(out[0:P, :], rows[:])

@@ -8,7 +8,6 @@ WORDS = 4096
 TOKENS = 4096
 N = 2048
 PIECE = 512
-WARM_UP = 5
 FLIP = 4
 BF16, F32, U16 = mybir.dt.bfloat16, mybir.dt.float32, mybir.dt.uint16
 
@@ -27,10 +26,8 @@ def tile_entattentionlayer_b_kernel(tc, x, table, wq, bq, wk, bk, wv, bv, offs, 
         tc.tile_pool(name="held", bufs=1) as held,
         tc.tile_pool(name="landing", bufs=n_groups) as landing,
         tc.tile_pool(name="staging", bufs=6) as staging,
-        tc.psum_pool(name="flip", bufs=2) as flip,
-        tc.psum_pool(name="banks", bufs=6) as banks,
     ):
-        table_groups = table.rearrange("(g b p) d -> g p b d", b=FLIP, p=P)
+        table_groups = table.rearrange("(g p b) d -> g p b d", b=FLIP, p=P)
         word_rows = []
         for g in range(n_groups):
             word_rows.append(landing.tile([P, FLIP, P], BF16, name="word_rows", tag="landing"))
@@ -50,81 +47,73 @@ def tile_entattentionlayer_b_kernel(tc, x, table, wq, bq, wk, bk, wv, bv, offs, 
         identity = held.tile([P, P], BF16, name="identity")
         masks.make_identity(nc, identity[:])
 
-        zeros = held.tile([P, PIECE], BF16, name="zeros")
-        nc.vector.memset(zeros[:], 0.0)
-
-        def keep_warm(moving):
-            unread = banks.tile([P, PIECE], F32, name="bank")
-            nc.tensor.matmul(unread[:], zeros[:, 0:P], moving, start=True, stop=True)
-
-        for w in range(WARM_UP):
-            keep_warm(zeros[:])
-
         window = held.tile([P, WORDS], BF16, name="window")
-        for g in range(n_groups):
-            flipped = flip.tile([P, FLIP * P], BF16, name="flipped")
-            for b in range(FLIP):
-                nc.tensor.transpose(flipped[:, b * P : (b + 1) * P], word_rows[g][:, b, :], identity[:])
-            keep_warm(word_rows[g][:].rearrange("p b d -> p (b d)"))
-            cols = slice(g * FLIP * P, (g + 1) * FLIP * P)
-            if g % 2 == 0:
-                nc.vector.tensor_copy(window[:, cols], flipped[:])
-            else:
-                nc.scalar.copy(window[:, cols], flipped[:])
+        with tc.psum_pool(name="flip", bufs=n_groups) as flip:
+            for g in range(n_groups):
+                flipped = flip.tile([P, FLIP * P], BF16, name="flipped")
+                for b in range(FLIP):
+                    nc.tensor.transpose(flipped[:, b * P : (b + 1) * P], word_rows[g][:, b, :], identity[:])
+                in_order = flipped[:].rearrange("d (b p) -> d p b", b=FLIP)
+                dest = window[:, g * FLIP * P : (g + 1) * FLIP * P].rearrange("d (p b) -> d p b", b=FLIP)
+                if g % 2 == 0:
+                    nc.vector.tensor_copy(dest, in_order)
+                else:
+                    nc.scalar.copy(dest, in_order)
 
         x_f32 = []
         for c in range(n_chunks):
             x_f32.append(landing.tile([P, PIECE], F32, name="x_f32", tag="landing"))
             nc.sync.dma_start(x_f32[c][:], x[:, c * PIECE : (c + 1) * PIECE])
 
-        def add_bias(turn, dest, bank, bias):
-            if turn % 2 == 0:
-                nc.vector.tensor_scalar(dest, bank, bias, None, add)
-            else:
-                nc.scalar.activation(dest, bank, identity_fn, bias=bias)
+        with tc.psum_pool(name="banks", bufs=8) as banks:
+            def add_bias(turn, dest, bank, bias):
+                if turn % 2 == 0:
+                    nc.vector.tensor_scalar(dest, bank, bias, None, add)
+                else:
+                    nc.scalar.activation(dest, bank, identity_fn, bias=bias)
 
-        def scale_down(turn, dest, bank):
-            if turn % 2 == 0:
-                nc.vector.tensor_scalar(dest, bank, inv_sqrt_d, None, mult)
-            else:
-                nc.scalar.activation(dest, bank, identity_fn, scale=inv_sqrt_d)
+            def scale_down(turn, dest, bank):
+                if turn % 2 == 0:
+                    nc.vector.tensor_scalar(dest, bank, inv_sqrt_d, None, mult)
+                else:
+                    nc.scalar.activation(dest, bank, identity_fn, scale=inv_sqrt_d)
 
-        x_bf = held.tile([P, TOKENS], BF16, name="x_bf")
-        q_bf = held.tile([P, TOKENS], BF16, name="q_bf")
+            x_bf = held.tile([P, TOKENS], BF16, name="x_bf")
+            q_bf = held.tile([P, TOKENS], BF16, name="q_bf")
 
-        def project_queries(c):
-            cols = slice(c * PIECE, (c + 1) * PIECE)
-            nc.gpsimd.tensor_copy(x_bf[:, cols], x_f32[c][:])
-            bank = banks.tile([P, PIECE], F32, name="bank")
-            nc.tensor.matmul(bank[:], weights["q"][:], x_bf[:, cols], start=True, stop=True)
-            add_bias(c, q_bf[:, cols], bank[:], biases["q"][:, 0:1])
-
-        def project_tags(name, j, dest):
-            looked_up = window[:].indirect(offsets[:, j * (PIECE // 16) : (j + 1) * (PIECE // 16)])
-            bank = banks.tile([P, PIECE], F32, name="bank")
-            nc.tensor.matmul(bank[:], weights[name][:], looked_up, start=True, stop=True)
-            add_bias(j, dest, bank[:], biases[name][:, 0:1])
-
-        project_queries(0)
-
-        k_bf = held.tile([P, N], BF16, name="k_bf")
-        for j in range(N // PIECE):
-            project_tags("k", j, k_bf[:, j * PIECE : (j + 1) * PIECE])
-
-        for t in range(TOKENS // P):
-            rows = staging.tile([P, N], F32, name="rows")
-            for j in range(N // PIECE):
-                cols = slice(j * PIECE, (j + 1) * PIECE)
+            def project_queries(c):
+                cols = slice(c * PIECE, (c + 1) * PIECE)
+                nc.gpsimd.tensor_copy(x_bf[:, cols], x_f32[c][:])
                 bank = banks.tile([P, PIECE], F32, name="bank")
-                nc.tensor.matmul(bank[:], q_bf[:, t * P : (t + 1) * P], k_bf[:, cols], start=True, stop=True)
-                scale_down(j, rows[:, cols], bank[:])
-            nc.sync.dma_start(out[P + t * P : P + (t + 1) * P, :], rows[:])
+                nc.tensor.matmul(bank[:], weights["q"][:], x_bf[:, cols], start=True, stop=True)
+                add_bias(c, q_bf[:, cols], bank[:], biases["q"][:, 0:1])
 
-            if t % (PIECE // P) == 0 and t // (PIECE // P) + 1 < n_chunks:
-                project_queries(t // (PIECE // P) + 1)
+            def project_tags(name, j, dest):
+                looked_up = window[:].indirect(offsets[:, j * (PIECE // 16) : (j + 1) * (PIECE // 16)])
+                bank = banks.tile([P, PIECE], F32, name="bank")
+                nc.tensor.matmul(bank[:], weights[name][:], looked_up, start=True, stop=True)
+                add_bias(j, dest, bank[:], biases[name][:, 0:1])
 
-            if t == 7:
+            project_queries(0)
+
+            k_bf = held.tile([P, N], BF16, name="k_bf")
+            for j in range(N // PIECE):
+                project_tags("k", j, k_bf[:, j * PIECE : (j + 1) * PIECE])
+
+            for t in range(TOKENS // P):
                 rows = staging.tile([P, N], F32, name="rows")
                 for j in range(N // PIECE):
-                    project_tags("v", j, rows[:, j * PIECE : (j + 1) * PIECE])
-                nc.sync.dma_start(out[0:P, :], rows[:])
+                    cols = slice(j * PIECE, (j + 1) * PIECE)
+                    bank = banks.tile([P, PIECE], F32, name="bank")
+                    nc.tensor.matmul(bank[:], q_bf[:, t * P : (t + 1) * P], k_bf[:, cols], start=True, stop=True)
+                    scale_down(j, rows[:, cols], bank[:])
+                nc.sync.dma_start(out[P + t * P : P + (t + 1) * P, :], rows[:])
+
+                if t % (PIECE // P) == 0 and t // (PIECE // P) + 1 < n_chunks:
+                    project_queries(t // (PIECE // P) + 1)
+
+                if t == 7:
+                    rows = staging.tile([P, N], F32, name="rows")
+                    for j in range(N // PIECE):
+                        project_tags("v", j, rows[:, j * PIECE : (j + 1) * PIECE])
+                    nc.sync.dma_start(out[0:P, :], rows[:])

@@ -8,6 +8,7 @@ WORDS = 4096
 TOKENS = 4096
 N = 2048
 PIECE = 512
+GROUP = PIECE // P
 FLIP = 4
 BF16, F32, U16 = mybir.dt.bfloat16, mybir.dt.float32, mybir.dt.uint16
 
@@ -25,7 +26,7 @@ def tile_entattentionlayer_b_kernel(tc, x, table, wq, bq, wk, bk, wv, bv, offs, 
     with (
         tc.tile_pool(name="held", bufs=1) as held,
         tc.tile_pool(name="landing", bufs=n_groups) as landing,
-        tc.tile_pool(name="staging", bufs=6) as staging,
+        tc.tile_pool(name="staging", bufs=3) as staging,
     ):
         table_groups = table.rearrange("(g p b) d -> g p b d", b=FLIP, p=P)
         word_rows = []
@@ -100,20 +101,26 @@ def tile_entattentionlayer_b_kernel(tc, x, table, wq, bq, wk, bk, wv, bv, offs, 
             for j in range(N // PIECE):
                 project_tags("k", j, k_bf[:, j * PIECE : (j + 1) * PIECE])
 
-            for t in range(TOKENS // P):
-                rows = staging.tile([P, N], F32, name="rows")
-                for j in range(N // PIECE):
-                    cols = slice(j * PIECE, (j + 1) * PIECE)
-                    bank = banks.tile([P, PIECE], F32, name="bank")
-                    nc.tensor.matmul(bank[:], q_bf[:, t * P : (t + 1) * P], k_bf[:, cols], start=True, stop=True)
-                    scale_down(j, rows[:, cols], bank[:])
-                nc.sync.dma_start(out[P + t * P : P + (t + 1) * P, :], rows[:])
-
-                if t % (PIECE // P) == 0 and t // (PIECE // P) + 1 < n_chunks:
-                    project_queries(t // (PIECE // P) + 1)
-
-                if t == 7:
-                    rows = staging.tile([P, N], F32, name="rows")
+            for c in range(n_chunks):
+                rows = staging.tile([P, GROUP, N], F32, name="rows")
+                out_rows = out[P + c * PIECE : P + (c + 1) * PIECE, :].rearrange("(p i) n -> p i n", i=GROUP)
+                q_chunk = q_bf[:, c * PIECE : (c + 1) * PIECE].rearrange("m (p i) -> m i p", i=GROUP)
+                by_row = c == 0 or c == n_chunks - 1
+                for i in range(GROUP):
                     for j in range(N // PIECE):
-                        project_tags("v", j, rows[:, j * PIECE : (j + 1) * PIECE])
-                    nc.sync.dma_start(out[0:P, :], rows[:])
+                        cols = slice(j * PIECE, (j + 1) * PIECE)
+                        bank = banks.tile([P, PIECE], F32, name="bank")
+                        nc.tensor.matmul(bank[:], q_chunk[:, i, :], k_bf[:, cols], start=True, stop=True)
+                        scale_down(j, rows[:, i, cols], bank[:])
+                    if by_row:
+                        nc.sync.dma_start(out_rows[:, i, :], rows[:, i, :])
+                    if i == 0 and c + 1 < n_chunks:
+                        project_queries(c + 1)
+                if not by_row:
+                    nc.sync.dma_start(out_rows, rows[:])
+
+                if c == 1:
+                    v_rows = held.tile([P, N], F32, name="v_rows")
+                    for j in range(N // PIECE):
+                        project_tags("v", j, v_rows[:, j * PIECE : (j + 1) * PIECE])
+                    nc.sync.dma_start(out[0:P, :], v_rows[:])

@@ -105,7 +105,7 @@ def tile_entattentionlayer_b_kernel(tc, x, table, wq, bq, wk, bk, wv, bv, offs, 
                 rows = staging.tile([P, GROUP, N], F32, name="rows")
                 out_rows = out[P + c * PIECE : P + (c + 1) * PIECE, :].rearrange("(p i) n -> p i n", i=GROUP)
                 q_chunk = q_bf[:, c * PIECE : (c + 1) * PIECE].rearrange("m (p i) -> m i p", i=GROUP)
-                by_row = c == 0 or c == n_chunks - 1
+                by_row = c == 0
                 for i in range(GROUP):
                     for j in range(N // PIECE):
                         cols = slice(j * PIECE, (j + 1) * PIECE)

@@ -10,6 +10,7 @@ N = 2048
 PIECE = 512
 GROUP = PIECE // P
 FLIP = 4
+PER_LOAD = 2
 BF16, F32, U16 = mybir.dt.bfloat16, mybir.dt.float32, mybir.dt.uint16
 
 FLOPS = 2 * P * P * (2 * N + TOKENS) + 2 * P * TOKENS * N
@@ -21,50 +22,59 @@ def tile_entattentionlayer_b_kernel(tc, x, table, wq, bq, wk, bk, wv, bv, offs, 
     add, mult = mybir.AluOpType.add, mybir.AluOpType.mult
     inv_sqrt_d = 1.0 / math.sqrt(P)
     n_groups = WORDS // P // FLIP
+    n_loads = n_groups // PER_LOAD
     n_chunks = TOKENS // PIECE
 
     with (
         tc.tile_pool(name="held", bufs=1) as held,
-        tc.tile_pool(name="landing", bufs=n_groups) as landing,
+        tc.tile_pool(name="landing", bufs=n_loads) as landing,
+        tc.tile_pool(name="tokens", bufs=n_chunks) as tokens,
         tc.tile_pool(name="staging", bufs=3) as staging,
     ):
-        table_groups = table.rearrange("(g p b) d -> g p b d", b=FLIP, p=P)
+        identity = held.tile([P, P], BF16, name="identity")
+        masks.make_identity(nc, identity[:])
+
+        table_loads = table.rearrange("(t h p b) d -> t p h b d", h=PER_LOAD, b=FLIP, p=P)
         word_rows = []
-        for g in range(n_groups):
-            word_rows.append(landing.tile([P, FLIP, P], BF16, name="word_rows", tag="landing"))
-            nc.sync.dma_start(word_rows[g][:], table_groups[g])
+        for t in range(n_loads):
+            word_rows.append(landing.tile([P, PER_LOAD, FLIP, P], BF16, name="word_rows"))
+            nc.sync.dma_start(word_rows[t][:], table_loads[t])
 
         offsets = held.tile([P, N // 16], U16, name="offsets")
         nc.sync.dma_start(offsets[:], offs)
 
         weights = {}
         biases = {}
-        for name, w_dram, b_dram in (("k", wk, bk), ("q", wq, bq), ("v", wv, bv)):
-            weights[name] = held.tile([P, P], BF16, name=f"w{name}")
-            nc.scalar.dma_start(weights[name][:], w_dram)
-            biases[name] = held.tile([P, 1], F32, name=f"b{name}")
-            nc.scalar.dma_start(biases[name][:], b_dram)
 
-        identity = held.tile([P, P], BF16, name="identity")
-        masks.make_identity(nc, identity[:])
+        def load_projection(name, w_dram, w_queue, b_dram, b_queue):
+            weights[name] = held.tile([P, P], BF16, name=f"w{name}")
+            w_queue.dma_start(weights[name][:], w_dram)
+            biases[name] = held.tile([P, 1], F32, name=f"b{name}")
+            b_queue.dma_start(biases[name][:], b_dram)
+
+        load_projection("k", wk, nc.scalar, bk, nc.gpsimd)
+        load_projection("q", wq, nc.scalar, bq, nc.gpsimd)
+
+        x_f32 = []
+        for c in range(n_chunks):
+            x_f32.append(tokens.tile([P, PIECE], F32, name="x_f32"))
+            nc.sync.dma_start(x_f32[c][:], x[:, c * PIECE : (c + 1) * PIECE])
+
+        load_projection("v", wv, nc.sync, bv, nc.sync)
 
         window = held.tile([P, WORDS], BF16, name="window")
         with tc.psum_pool(name="flip", bufs=n_groups) as flip:
             for g in range(n_groups):
                 flipped = flip.tile([P, FLIP * P], BF16, name="flipped")
                 for b in range(FLIP):
-                    nc.tensor.transpose(flipped[:, b * P : (b + 1) * P], word_rows[g][:, b, :], identity[:])
+                    block = word_rows[g // PER_LOAD][:, g % PER_LOAD, b, :]
+                    nc.tensor.transpose(flipped[:, b * P : (b + 1) * P], block, identity[:])
                 in_order = flipped[:].rearrange("d (b p) -> d p b", b=FLIP)
                 dest = window[:, g * FLIP * P : (g + 1) * FLIP * P].rearrange("d (p b) -> d p b", b=FLIP)
                 if g % 2 == 0:
                     nc.vector.tensor_copy(dest, in_order)
                 else:
                     nc.scalar.copy(dest, in_order)
-
-        x_f32 = []
-        for c in range(n_chunks):
-            x_f32.append(landing.tile([P, PIECE], F32, name="x_f32", tag="landing"))
-            nc.sync.dma_start(x_f32[c][:], x[:, c * PIECE : (c + 1) * PIECE])
 
         with tc.psum_pool(name="banks", bufs=8) as banks:
             def add_bias(turn, dest, bank, bias):
@@ -105,18 +115,19 @@ def tile_entattentionlayer_b_kernel(tc, x, table, wq, bq, wk, bk, wv, bv, offs, 
                 rows = staging.tile([P, GROUP, N], F32, name="rows")
                 out_rows = out[P + c * PIECE : P + (c + 1) * PIECE, :].rearrange("(p i) n -> p i n", i=GROUP)
                 q_chunk = q_bf[:, c * PIECE : (c + 1) * PIECE].rearrange("m (p i) -> m i p", i=GROUP)
-                by_row = c == 0
                 for i in range(GROUP):
+                    pieces_a_store = min(2**i, N // PIECE) if c == 0 else GROUP * N // PIECE
                     for j in range(N // PIECE):
                         cols = slice(j * PIECE, (j + 1) * PIECE)
                         bank = banks.tile([P, PIECE], F32, name="bank")
                         nc.tensor.matmul(bank[:], q_chunk[:, i, :], k_bf[:, cols], start=True, stop=True)
                         scale_down(j, rows[:, i, cols], bank[:])
-                    if by_row:
-                        nc.sync.dma_start(out_rows[:, i, :], rows[:, i, :])
+                        if (j + 1) % pieces_a_store == 0:
+                            ready = slice((j + 1 - pieces_a_store) * PIECE, (j + 1) * PIECE)
+                            nc.sync.dma_start(out_rows[:, i, ready], rows[:, i, ready])
                     if i == 0 and c + 1 < n_chunks:
                         project_queries(c + 1)
-                if not by_row:
+                if c > 0:
                     nc.sync.dma_start(out_rows, rows[:])
 
                 if c == 1:

import math

import concourse.masks as masks
import concourse.mybir as mybir

P = 128
WORDS = 4096
TOKENS = 4096
N = 2048
PIECE = 512
GROUP = PIECE // P
FLIP = 4
PER_LOAD = 2
BF16, F32, U16 = mybir.dt.bfloat16, mybir.dt.float32, mybir.dt.uint16

FLOPS = 2 * P * P * (2 * N + TOKENS) + 2 * P * TOKENS * N


def tile_entattentionlayer_b_kernel(tc, x, table, wq, bq, wk, bk, wv, bv, offs, out):
    nc = tc.nc
    identity_fn = mybir.ActivationFunctionType.Identity
    add, mult = mybir.AluOpType.add, mybir.AluOpType.mult
    inv_sqrt_d = 1.0 / math.sqrt(P)
    n_groups = WORDS // P // FLIP
    n_loads = n_groups // PER_LOAD
    n_chunks = TOKENS // PIECE

    with (
        tc.tile_pool(name="held", bufs=1) as held,
        tc.tile_pool(name="landing", bufs=n_loads) as landing,
        tc.tile_pool(name="tokens", bufs=n_chunks) as tokens,
        tc.tile_pool(name="staging", bufs=3) as staging,
    ):
        identity = held.tile([P, P], BF16, name="identity")
        masks.make_identity(nc, identity[:])

        table_loads = table.rearrange("(t h p b) d -> t p h b d", h=PER_LOAD, b=FLIP, p=P)
        word_rows = []
        for t in range(n_loads):
            word_rows.append(landing.tile([P, PER_LOAD, FLIP, P], BF16, name="word_rows"))
            nc.sync.dma_start(word_rows[t][:], table_loads[t])

        offsets = held.tile([P, N // 16], U16, name="offsets")
        nc.sync.dma_start(offsets[:], offs)

        weights = {}
        biases = {}

        def load_projection(name, w_dram, w_queue, b_dram, b_queue):
            weights[name] = held.tile([P, P], BF16, name=f"w{name}")
            w_queue.dma_start(weights[name][:], w_dram)
            biases[name] = held.tile([P, 1], F32, name=f"b{name}")
            b_queue.dma_start(biases[name][:], b_dram)

        load_projection("k", wk, nc.scalar, bk, nc.gpsimd)
        load_projection("q", wq, nc.scalar, bq, nc.gpsimd)

        x_f32 = []
        for c in range(n_chunks):
            x_f32.append(tokens.tile([P, PIECE], F32, name="x_f32"))
            nc.sync.dma_start(x_f32[c][:], x[:, c * PIECE : (c + 1) * PIECE])

        load_projection("v", wv, nc.sync, bv, nc.sync)

        window = held.tile([P, WORDS], BF16, name="window")
        with tc.psum_pool(name="flip", bufs=n_groups) as flip:
            for g in range(n_groups):
                flipped = flip.tile([P, FLIP * P], BF16, name="flipped")
                for b in range(FLIP):
                    block = word_rows[g // PER_LOAD][:, g % PER_LOAD, b, :]
                    nc.tensor.transpose(flipped[:, b * P : (b + 1) * P], block, identity[:])
                in_order = flipped[:].rearrange("d (b p) -> d p b", b=FLIP)
                dest = window[:, g * FLIP * P : (g + 1) * FLIP * P].rearrange("d (p b) -> d p b", b=FLIP)
                if g % 2 == 0:
                    nc.vector.tensor_copy(dest, in_order)
                else:
                    nc.scalar.copy(dest, in_order)

        with tc.psum_pool(name="banks", bufs=8) as banks:
            def add_bias(turn, dest, bank, bias):
                if turn % 2 == 0:
                    nc.vector.tensor_scalar(dest, bank, bias, None, add)
                else:
                    nc.scalar.activation(dest, bank, identity_fn, bias=bias)

            def scale_down(turn, dest, bank):
                if turn % 2 == 0:
                    nc.vector.tensor_scalar(dest, bank, inv_sqrt_d, None, mult)
                else:
                    nc.scalar.activation(dest, bank, identity_fn, scale=inv_sqrt_d)

            x_bf = held.tile([P, TOKENS], BF16, name="x_bf")
            q_bf = held.tile([P, TOKENS], BF16, name="q_bf")

            def project_queries(c):
                cols = slice(c * PIECE, (c + 1) * PIECE)
                nc.gpsimd.tensor_copy(x_bf[:, cols], x_f32[c][:])
                bank = banks.tile([P, PIECE], F32, name="bank")
                nc.tensor.matmul(bank[:], weights["q"][:], x_bf[:, cols], start=True, stop=True)
                add_bias(c, q_bf[:, cols], bank[:], biases["q"][:, 0:1])

            def project_tags(name, j, dest):
                looked_up = window[:].indirect(offsets[:, j * (PIECE // 16) : (j + 1) * (PIECE // 16)])
                bank = banks.tile([P, PIECE], F32, name="bank")
                nc.tensor.matmul(bank[:], weights[name][:], looked_up, start=True, stop=True)
                add_bias(j, dest, bank[:], biases[name][:, 0:1])

            project_queries(0)

            k_bf = held.tile([P, N], BF16, name="k_bf")
            for j in range(N // PIECE):
                project_tags("k", j, k_bf[:, j * PIECE : (j + 1) * PIECE])

            for c in range(n_chunks):
                rows = staging.tile([P, GROUP, N], F32, name="rows")
                out_rows = out[P + c * PIECE : P + (c + 1) * PIECE, :].rearrange("(p i) n -> p i n", i=GROUP)
                q_chunk = q_bf[:, c * PIECE : (c + 1) * PIECE].rearrange("m (p i) -> m i p", i=GROUP)
                for i in range(GROUP):
                    pieces_a_store = min(2**i, N // PIECE) if c == 0 else GROUP * N // PIECE
                    for j in range(N // PIECE):
                        cols = slice(j * PIECE, (j + 1) * PIECE)
                        bank = banks.tile([P, PIECE], F32, name="bank")
                        nc.tensor.matmul(bank[:], q_chunk[:, i, :], k_bf[:, cols], start=True, stop=True)
                        scale_down(j, rows[:, i, cols], bank[:])
                        if (j + 1) % pieces_a_store == 0:
                            ready = slice((j + 1 - pieces_a_store) * PIECE, (j + 1) * PIECE)
                            nc.sync.dma_start(out_rows[:, i, ready], rows[:, i, ready])
                    if i == 0 and c + 1 < n_chunks:
                        project_queries(c + 1)
                if c > 0:
                    nc.sync.dma_start(out_rows, rows[:])

                if c == 1:
                    v_rows = held.tile([P, N], F32, name="v_rows")
                    for j in range(N // PIECE):
                        project_tags("v", j, v_rows[:, j * PIECE : (j + 1) * PIECE])
                    nc.sync.dma_start(out[0:P, :], v_rows[:])
